import numpy as np
import ml_dtypes


def mxq(x, axis, fmt="e4m3"):
    dtype, down = {"e4m3": (ml_dtypes.float8_e4m3fn, 7), "e5m2": (ml_dtypes.float8_e5m2, 14)}[fmt]
    v = np.moveaxis(np.asarray(x, np.float32).astype(ml_dtypes.bfloat16).astype(np.float64), axis, -1)
    blocks = v.reshape(v.shape[:-1] + (-1, 32))
    amax = np.abs(blocks).max(-1, keepdims=True)
    byte = np.maximum(np.where(amax > 0, np.frexp(amax)[1] - 1 + 127, 0) - down, 1)
    scale = np.exp2(byte - 127.0)
    codes = (blocks / scale).astype(np.float32).astype(dtype).astype(np.float64)
    return np.moveaxis((codes * scale).reshape(v.shape), -1, axis)


WIDE = False


def mx_kscale(k):
    if not WIDE:
        return np.ones(k)
    levels = np.array([10, -10, 5, -5, 0])
    a = np.random.permutation(np.resize(levels, k // 512 * 4)).reshape(k // 512, 4)
    idx = np.arange(k)
    return np.exp2(a[idx // 512, idx % 128 // 32])


BF16 = ml_dtypes.bfloat16


def bf(x):
    return np.asarray(x, np.float32).astype(BF16)


def f64(x):
    return np.asarray(x).astype(np.float64)


E2M1 = np.array([0.0, 0.5, 1.0, 1.5, 2.0, 3.0, 4.0, 6.0, -0.0, -0.5, -1.0, -1.5, -2.0, -3.0, -4.0, -6.0])


def pack_weight(w, fmt):
    k, n = w.shape
    w = f64(bf(w)).reshape(k // 32, 32, n)
    amax = np.abs(w).max(1)
    if fmt == "e4m3":
        byte = np.frexp(amax)[1] - 1 + 127 - 7
    else:
        mant, ex = np.frexp(amax / 6.0)
        byte = np.where(mant > 0.5, ex, ex - 1) + 127
    byte = np.clip(np.where(amax > 0, byte, 1), 1, 254)
    scaled = (w * np.exp2(127.0 - byte)[:, None, :]).reshape(k, n).astype(np.float32)
    by_word = np.ascontiguousarray(scaled.reshape(k // 512, 128, 4, n).transpose(0, 1, 3, 2))
    if fmt == "e4m3":
        words = by_word.astype(ml_dtypes.float8_e4m3fn).view(np.uint8)
    else:
        c = by_word.astype(ml_dtypes.float4_e2m1fn).view(np.uint8) & 0xF
        words = c[..., 0::2] | (c[..., 1::2] << 4)
    return np.ascontiguousarray(words), np.ascontiguousarray(byte.astype(np.uint8).reshape(k // 512, 16, n))


def unpack_weight(words, scales, fmt):
    g, p, n, _ = words.shape
    if fmt == "e4m3":
        vals = np.ascontiguousarray(words).view(ml_dtypes.float8_e4m3fn).astype(np.float64)
    else:
        nib = np.empty((g, p, n, 4), np.uint8)
        nib[..., 0::2] = words & 0xF
        nib[..., 1::2] = words >> 4
        vals = E2M1[nib]
    vals = vals * np.repeat(np.exp2(scales.astype(np.float64) - 127.0), 8, axis=1)[..., None]
    return vals.transpose(0, 1, 3, 2).reshape(g * 512, n)


I, M, O, B = 1024, 1024, 1024, 1024
FMT = "e4m3"


def sigmoid(v):
    return 1.0 / (1.0 + np.exp(-v))


def setup_inputs():
    s, u, t = mx_kscale(I), mx_kscale(O), mx_kscale(M)
    x = bf(np.random.standard_normal((I, B)) * s[:, None])
    out0 = bf(np.tanh(np.random.standard_normal((O, B))) * u[:, None])
    mem0 = bf(np.random.standard_normal((M, B)) * 0.8 * t[:, None])
    w_inp_words, w_inp_scales = pack_weight((np.random.standard_normal((M, I)) / np.sqrt(I) / s).T, FMT)
    w_rec_inp_words, w_rec_inp_scales = pack_weight((np.random.standard_normal((M, O)) / np.sqrt(O) / u).T, FMT)
    w_inpgate_words, w_inpgate_scales = pack_weight((np.random.standard_normal((M, I)) / np.sqrt(I) / s).T, FMT)
    w_mem_inpgate_words, w_mem_inpgate_scales = pack_weight((np.random.standard_normal((M, M)) / np.sqrt(M) / t).T, FMT)
    w_rec_inpgate_words, w_rec_inpgate_scales = pack_weight((np.random.standard_normal((M, O)) / np.sqrt(O) / u).T, FMT)
    return {
        "x": x,
        "out0": out0,
        "mem0": mem0,
        "w_inp_words": w_inp_words,
        "w_inp_scales": w_inp_scales,
        "w_rec_inp_words": w_rec_inp_words,
        "w_rec_inp_scales": w_rec_inp_scales,
        "w_inpgate_words": w_inpgate_words,
        "w_inpgate_scales": w_inpgate_scales,
        "w_mem_inpgate_words": w_mem_inpgate_words,
        "w_mem_inpgate_scales": w_mem_inpgate_scales,
        "w_rec_inpgate_words": w_rec_inpgate_words,
        "w_rec_inpgate_scales": w_rec_inpgate_scales,
    }


def reference(x, out0, mem0, w_inp_words, w_inp_scales, w_rec_inp_words, w_rec_inp_scales, w_inpgate_words, w_inpgate_scales, w_mem_inpgate_words, w_mem_inpgate_scales, w_rec_inpgate_words, w_rec_inpgate_scales):
    xq = mxq(f64(x), 0, "e4m3")
    oq = mxq(f64(out0), 0, "e4m3")
    mq = mxq(f64(mem0), 0, "e4m3")
    block_inp = sigmoid((unpack_weight(w_inp_words, w_inp_scales, FMT).T @ xq) + (unpack_weight(w_rec_inp_words, w_rec_inp_scales, FMT).T @ oq))
    inp_gate = sigmoid((unpack_weight(w_inpgate_words, w_inpgate_scales, FMT).T @ xq) + (unpack_weight(w_mem_inpgate_words, w_mem_inpgate_scales, FMT).T @ mq) + (unpack_weight(w_rec_inpgate_words, w_rec_inpgate_scales, FMT).T @ oq))
    return block_inp * inp_gate

@@ -1,0 +1,207 @@
+from contextlib import ExitStack
+
+import concourse.mybir as mybir
+
+BF16 = mybir.dt.bfloat16
+F32 = mybir.dt.float32
+I32 = mybir.dt.int32
+U32 = mybir.dt.uint32
+U8 = mybir.dt.uint8
+FP8X4 = mybir.dt.float8_e4m3fn_x4
+SIGMOID = mybir.ActivationFunctionType.Sigmoid
+
+P = 128
+PACK = 4
+K_PASS = P * PACK
+FEATURES = 1024
+BATCH = 1024
+GROUPS = FEATURES // K_PASS
+N_TILES = FEATURES // P
+HALF = 512
+HALVES = BATCH // HALF
+QUADRANTS = 4
+RUN = 4
+
+FLOPS = 5 * 2 * FEATURES * FEATURES * BATCH
+
+BLOCK_TERMS = (("inp", "x"), ("rec_inp", "out0"))
+GATE_TERMS = (("inpgate", "x"), ("rec_inpgate", "out0"), ("mem_inpgate", "mem0"))
+
+
+def tile_pt_grumb_pa_kernel(
+    tc,
+    x,
+    out0,
+    mem0,
+    w_inp_words,
+    w_inp_scales,
+    w_rec_inp_words,
+    w_rec_inp_scales,
+    w_inpgate_words,
+    w_inpgate_scales,
+    w_mem_inpgate_words,
+    w_mem_inpgate_scales,
+    w_rec_inpgate_words,
+    w_rec_inpgate_scales,
+    out,
+):
+    nc = tc.nc
+    activations = {"x": x, "out0": out0, "mem0": mem0}
+    words_in = {
+        "inp": w_inp_words,
+        "rec_inp": w_rec_inp_words,
+        "inpgate": w_inpgate_words,
+        "mem_inpgate": w_mem_inpgate_words,
+        "rec_inpgate": w_rec_inpgate_words,
+    }
+    scales_in = {
+        "inp": w_inp_scales,
+        "rec_inp": w_rec_inp_scales,
+        "inpgate": w_inpgate_scales,
+        "mem_inpgate": w_mem_inpgate_scales,
+        "rec_inpgate": w_rec_inpgate_scales,
+    }
+
+    with ExitStack() as ctx:
+        ctx.enter_context(tc.manual_schedule())
+        keep = ctx.enter_context(tc.tile_pool(name="keep", bufs=1))
+        stage = ctx.enter_context(tc.tile_pool(name="stage", bufs=3))
+        psum = ctx.enter_context(tc.psum_pool(name="psum", bufs=8))
+
+        raw = {}
+        act_codes = {}
+        act_scales = {}
+        w_codes = {}
+        w_scales = {}
+        block_sig = {}
+
+        def load_activation(a, g, h):
+            raw[(a, g, h)] = keep.tile([P, PACK, HALF], BF16, name="raw_%s_%d_%d" % (a, g, h))
+            rows = activations[a][g * K_PASS : (g + 1) * K_PASS, h * HALF : (h + 1) * HALF]
+            nc.sync.dma_start(
+                out=raw[(a, g, h)][:], in_=rows.rearrange("(p t) c -> p t c", t=PACK)
+            )
+
+        def load_weight_scales(w):
+            for quadrant in range(QUADRANTS):
+                nc.sync.dma_start(
+                    out=w_scales[w][32 * quadrant : 32 * quadrant + GROUPS * 4, :].bitcast(I32),
+                    in_=scales_in[w][:, 4 * quadrant : 4 * quadrant + 4, :].bitcast(I32),
+                )
+
+        def load_weight_codes(w, g):
+            w_codes[(w, g)] = keep.tile(
+                [P, FEATURES], U32, name="w_codes_%s_%d" % (w, g), align_bytes=64
+            )
+            nc.sync.dma_start(
+                out=w_codes[(w, g)][:].bitcast(I32),
+                in_=words_in[w][g].rearrange("p n t -> p (n t)").bitcast(I32),
+            )
+
+        def quantise(a, g, h):
+            grouped = stage.tile([P, HALF, PACK], BF16, align_bytes=64)
+            nc.vector.tensor_copy(
+                out=grouped[:].rearrange("p (c i) t -> p c t i", i=RUN),
+                in_=raw[(a, g, h)][:].rearrange("p t (c i) -> p c t i", i=RUN),
+            )
+            act_codes[(a, g, h)] = keep.tile(
+                [P, HALF], U32, name="act_codes_%s_%d_%d" % (a, g, h), align_bytes=64
+            )
+            act_scales[(a, g, h)] = keep.tile(
+                [P, HALF], U8, name="act_scales_%s_%d_%d" % (a, g, h), align_bytes=64
+            )
+            nc.vector.quantize_mx(
+                out=act_codes[(a, g, h)][:].bitcast(FP8X4),
+                scales=act_scales[(a, g, h)][:],
+                in_=grouped[:].rearrange("p c t -> p (c t)"),
+            )
+
+        def run_round(terms, h, visits, finish):
+            last = len(terms) * GROUPS - 1
+            banks = {}
+            for n, c in visits:
+                w, a = terms[c // GROUPS]
+                g = c % GROUPS
+                if c == 0:
+                    banks[n] = psum.tile([P, HALF], F32, name="bank")
+                n_cols = slice(n * P, (n + 1) * P)
+                nc.tensor.matmul_mx(
+                    out=banks[n][:],
+                    lhsT=w_codes[(w, g)][:, n_cols].bitcast(FP8X4),
+                    lhsT_scale=w_scales[w][4 * g : P, n_cols],
+                    rhs=act_codes[(a, g, h)][:].bitcast(FP8X4),
+                    rhs_scale=act_scales[(a, g, h)][:],
+                    start=(c == 0),
+                    stop=(c == last),
+                )
+                if c == last:
+                    finish(n, h, banks[n])
+
+        def finish_block(n, h, bank):
+            block_sig[(n, h)] = keep.tile([P, HALF], F32, name="block_sig_%d_%d" % (n, h))
+            nc.scalar.activation(out=block_sig[(n, h)][:], in_=bank[:], func=SIGMOID)
+
+        def finish_gate(n, h, bank):
+            result = keep.tile([P, HALF], F32, name="result_%d_%d" % (n, h))
+            nc.scalar.activation(out=result[:], in_=bank[:], func=SIGMOID)
+            nc.vector.tensor_mul(out=result[:], in0=result[:], in1=block_sig[(n, h)][:])
+            nc.sync.dma_start(
+                out=out[n * P : (n + 1) * P, h * HALF : (h + 1) * HALF], in_=result[:]
+            )
+
+        for w, a in BLOCK_TERMS + GATE_TERMS:
+            w_scales[w] = keep.tile([P, FEATURES], U8, name="w_scales_%s" % w, align_bytes=64)
+            nc.vector.memset(w_scales[w][:].bitcast(I32), 0)
+
+        load_activation("x", 0, 0)
+        load_weight_scales("inp")
+        load_weight_codes("inp", 0)
+        load_activation("x", 1, 0)
+        load_weight_codes("inp", 1)
+        load_weight_scales("rec_inp")
+        for g in range(GROUPS):
+            load_activation("out0", g, 0)
+            load_weight_codes("rec_inp", g)
+        for w in ("inpgate", "rec_inpgate"):
+            load_weight_scales(w)
+            for g in range(GROUPS):
+                load_weight_codes(w, g)
+        for g in range(GROUPS):
+            load_activation("mem0", g, 0)
+        load_weight_scales("mem_inpgate")
+        for g in range(GROUPS):
+            load_weight_codes("mem_inpgate", g)
+        for a in ("x", "out0", "mem0"):
+            for g in range(GROUPS):
+                load_activation(a, g, 1)
+
+        for h in range(HALVES):
+            for a in ("x", "out0", "mem0"):
+                for g in range(GROUPS):
+                    quantise(a, g, h)
+
+        tiles = range(N_TILES)
+        run_round(
+            BLOCK_TERMS,
+            0,
+            [(n, c) for c in range(len(BLOCK_TERMS) * GROUPS) for n in tiles],
+            finish_block,
+        )
+        run_round(
+            GATE_TERMS,
+            0,
+            [(n, GROUPS * t + g) for t in range(len(GATE_TERMS)) for n in tiles for g in range(GROUPS)],
+            finish_gate,
+        )
+        run_round(
+            BLOCK_TERMS,
+            1,
+            [(n, GROUPS * t + g) for t in range(len(BLOCK_TERMS)) for n in tiles for g in range(GROUPS)],
+            finish_block,
+        )
+        run_round(
+            GATE_TERMS,
+            1,
+            [(n, c) for n in tiles for c in range(len(GATE_TERMS) * GROUPS)],
+            finish_gate,
+        )

@@ -21,6 +21,8 @@ HALF = 512
 HALVES = BATCH // HALF
 QUADRANTS = 4
 RUN = 4
+SCALAR_COLS = HALF // 3 // RUN * RUN
+VECTOR_COLS = HALF - SCALAR_COLS
 
 FLOPS = 5 * 2 * FEATURES * FEATURES * BATCH
 
@@ -82,11 +84,11 @@ def tile_pt_grumb_pa_kernel(
                 out=raw[(a, g, h)][:], in_=rows.rearrange("(p t) c -> p t c", t=PACK)
             )
 
-        def load_weight_scales(w):
+        def load_weight_scales(w, queue, word):
             for quadrant in range(QUADRANTS):
-                nc.sync.dma_start(
-                    out=w_scales[w][32 * quadrant : 32 * quadrant + GROUPS * 4, :].bitcast(I32),
-                    in_=scales_in[w][:, 4 * quadrant : 4 * quadrant + 4, :].bitcast(I32),
+                queue.dma_start(
+                    out=w_scales[w][32 * quadrant : 32 * quadrant + GROUPS * 4, :].bitcast(word),
+                    in_=scales_in[w][:, 4 * quadrant : 4 * quadrant + 4, :].bitcast(word),
                 )
 
         def load_weight_codes(w, g):
@@ -98,12 +100,18 @@ def tile_pt_grumb_pa_kernel(
                 in_=words_in[w][g].rearrange("p n t -> p (n t)").bitcast(I32),
             )
 
-        def quantise(a, g, h):
+        def quantise(a, g, h, scalar_helps):
             grouped = stage.tile([P, HALF, PACK], BF16, align_bytes=64)
+            vector_cols = VECTOR_COLS if scalar_helps else HALF
             nc.vector.tensor_copy(
-                out=grouped[:].rearrange("p (c i) t -> p c t i", i=RUN),
-                in_=raw[(a, g, h)][:].rearrange("p t (c i) -> p c t i", i=RUN),
+                out=grouped[:, :vector_cols, :].rearrange("p (c i) t -> p c t i", i=RUN),
+                in_=raw[(a, g, h)][:, :, :vector_cols].rearrange("p t (c i) -> p c t i", i=RUN),
             )
+            if scalar_helps:
+                nc.scalar.copy(
+                    out=grouped[:, vector_cols:, :].rearrange("p (c i) t -> p c t i", i=RUN),
+                    in_=raw[(a, g, h)][:, :, vector_cols:].rearrange("p t (c i) -> p c t i", i=RUN),
+                )
             act_codes[(a, g, h)] = keep.tile(
                 [P, HALF], U32, name="act_codes_%s_%d_%d" % (a, g, h), align_bytes=64
             )
@@ -154,21 +162,20 @@ def tile_pt_grumb_pa_kernel(
             nc.vector.memset(w_scales[w][:].bitcast(I32), 0)
 
         load_activation("x", 0, 0)
-        load_weight_scales("inp")
+        load_weight_scales("inp", nc.sync, I32)
+        for w in ("rec_inp", "inpgate", "rec_inpgate", "mem_inpgate"):
+            load_weight_scales(w, nc.gpsimd, F32)
         load_weight_codes("inp", 0)
         load_activation("x", 1, 0)
         load_weight_codes("inp", 1)
-        load_weight_scales("rec_inp")
         for g in range(GROUPS):
             load_activation("out0", g, 0)
             load_weight_codes("rec_inp", g)
         for w in ("inpgate", "rec_inpgate"):
-            load_weight_scales(w)
             for g in range(GROUPS):
                 load_weight_codes(w, g)
         for g in range(GROUPS):
             load_activation("mem0", g, 0)
-        load_weight_scales("mem_inpgate")
         for g in range(GROUPS):
             load_weight_codes("mem_inpgate", g)
         for a in ("x", "out0", "mem0"):
@@ -178,7 +185,7 @@ def tile_pt_grumb_pa_kernel(
         for h in range(HALVES):
             for a in ("x", "out0", "mem0"):
                 for g in range(GROUPS):
-                    quantise(a, g, h)
+                    quantise(a, g, h, scalar_helps=(h == 0 and a != "mem0"))
 
         tiles = range(N_TILES)
         run_round(

@@ -24,6 +24,8 @@ RUN = 4
 SCALAR_COLS = HALF // 3 // RUN * RUN
 VECTOR_COLS = HALF - SCALAR_COLS
 
+WARM_MATMULS = 8
+
 FLOPS = 5 * 2 * FEATURES * FEATURES * BATCH
 
 BLOCK_TERMS = (("inp", "x"), ("rec_inp", "out0"))
@@ -157,7 +159,19 @@ def tile_pt_grumb_pa_kernel(
                 out=out[n * P : (n + 1) * P, h * HALF : (h + 1) * HALF], in_=result[:]
             )
 
-        for w, a in BLOCK_TERMS + GATE_TERMS:
+        w_scales["inp"] = keep.tile([P, FEATURES], U8, name="w_scales_inp", align_bytes=64)
+        nc.vector.memset(w_scales["inp"][:].bitcast(I32), 0)
+        warm = keep.tile([P, HALF], BF16, name="warm")
+        nc.vector.memset(warm[:], 1.0)
+        warm_sig = keep.tile([P, 1], F32, name="warm_sig")
+        nc.scalar.activation(out=warm_sig[:], in_=warm[:, 0:1], func=SIGMOID)
+        warm_bank = psum.tile([P, HALF], F32, name="bank")
+        for i in range(WARM_MATMULS):
+            nc.tensor.matmul(
+                out=warm_bank[:], lhsT=warm[:, :P], rhs=warm[:], start=True, stop=True
+            )
+
+        for w, a in BLOCK_TERMS[1:] + GATE_TERMS:
             w_scales[w] = keep.tile([P, FEATURES], U8, name="w_scales_%s" % w, align_bytes=64)
             nc.vector.memset(w_scales[w][:].bitcast(I32), 0)
 

@@ -24,6 +24,7 @@ RUN = 4
 SCALAR_COLS = HALF // 3 // RUN * RUN
 VECTOR_COLS = HALF - SCALAR_COLS
 
+LAST_WIDTHS = (256, 128, 128)
 WARM_MATMULS = 8
 
 FLOPS = 5 * 2 * FEATURES * FEATURES * BATCH
@@ -147,6 +148,33 @@ def tile_pt_grumb_pa_kernel(
                 if c == last:
                     finish(n, h, banks[n])
 
+        def run_last_tile(terms, n, h):
+            last = len(terms) * GROUPS - 1
+            n_cols = slice(n * P, (n + 1) * P)
+            first = 0
+            for width in LAST_WIDTHS:
+                cols = slice(first, first + width)
+                bank = psum.tile([P, width], F32, name="bank")
+                result = keep.tile([P, width], F32, name="result_%d_%d_%d" % (n, h, first))
+                for c in range(last + 1):
+                    w, a = terms[c // GROUPS]
+                    g = c % GROUPS
+                    nc.tensor.matmul_mx(
+                        out=bank[:],
+                        lhsT=w_codes[(w, g)][:, n_cols].bitcast(FP8X4),
+                        lhsT_scale=w_scales[w][4 * g : P, n_cols],
+                        rhs=act_codes[(a, g, h)][:, cols].bitcast(FP8X4),
+                        rhs_scale=act_scales[(a, g, h)][:, cols],
+                        start=(c == 0),
+                        stop=(c == last),
+                    )
+                nc.scalar.activation(out=result[:], in_=bank[:], func=SIGMOID)
+                nc.vector.tensor_mul(out=result[:], in0=result[:], in1=block_sig[(n, h)][:, cols])
+                nc.sync.dma_start(
+                    out=out[n_cols, h * HALF + first : h * HALF + first + width], in_=result[:]
+                )
+                first += width
+
         def finish_block(n, h, bank):
             block_sig[(n, h)] = keep.tile([P, HALF], F32, name="block_sig_%d_%d" % (n, h))
             nc.scalar.activation(out=block_sig[(n, h)][:], in_=bank[:], func=SIGMOID)
@@ -223,6 +251,7 @@ def tile_pt_grumb_pa_kernel(
         run_round(
             GATE_TERMS,
             1,
-            [(n, c) for n in tiles for c in range(len(GATE_TERMS) * GROUPS)],
+            [(n, c) for n in tiles[:-1] for c in range(len(GATE_TERMS) * GROUPS)],
             finish_gate,
         )
+        run_last_tile(GATE_TERMS, tiles[-1], 1)

@@ -94,13 +94,16 @@ def tile_pt_grumb_pa_kernel(
                     in_=scales_in[w][:, 4 * quadrant : 4 * quadrant + 4, :].bitcast(word),
                 )
 
-        def load_weight_codes(w, g):
-            w_codes[(w, g)] = keep.tile(
-                [P, FEATURES], U32, name="w_codes_%s_%d" % (w, g), align_bytes=64
-            )
+        def load_weight_codes(w, g, first=0, width=FEATURES):
+            if first == 0:
+                w_codes[(w, g)] = keep.tile(
+                    [P, FEATURES], U32, name="w_codes_%s_%d" % (w, g), align_bytes=64
+                )
             nc.sync.dma_start(
-                out=w_codes[(w, g)][:].bitcast(I32),
-                in_=words_in[w][g].rearrange("p n t -> p (n t)").bitcast(I32),
+                out=w_codes[(w, g)][:, first : first + width].bitcast(I32),
+                in_=words_in[w][g, :, first : first + width, :]
+                .rearrange("p n t -> p (n t)")
+                .bitcast(I32),
             )
 
         def quantise(a, g, h, scalar_helps):
@@ -203,16 +206,22 @@ def tile_pt_grumb_pa_kernel(
             w_scales[w] = keep.tile([P, FEATURES], U8, name="w_scales_%s" % w, align_bytes=64)
             nc.vector.memset(w_scales[w][:].bitcast(I32), 0)
 
+        low, high = (0, FEATURES // 2), (FEATURES // 2, FEATURES // 2)
         load_activation("x", 0, 0)
+        load_weight_codes("inp", 0, *low)
         load_weight_scales("inp", nc.sync, I32)
         for w in ("rec_inp", "inpgate", "rec_inpgate", "mem_inpgate"):
             load_weight_scales(w, nc.gpsimd, F32)
-        load_weight_codes("inp", 0)
         load_activation("x", 1, 0)
-        load_weight_codes("inp", 1)
-        for g in range(GROUPS):
-            load_activation("out0", g, 0)
-            load_weight_codes("rec_inp", g)
+        load_weight_codes("inp", 0, *high)
+        load_weight_codes("inp", 1, *low)
+        load_activation("out0", 0, 0)
+        load_weight_codes("inp", 1, *high)
+        load_weight_codes("rec_inp", 0, *low)
+        load_activation("out0", 1, 0)
+        load_weight_codes("rec_inp", 0, *high)
+        load_weight_codes("rec_inp", 1, *low)
+        load_weight_codes("rec_inp", 1, *high)
         for w in ("inpgate", "rec_inpgate"):
             for g in range(GROUPS):
                 load_weight_codes(w, g)

@@ -24,6 +24,7 @@ RUN = 4
 SCALAR_COLS = HALF // 3 // RUN * RUN
 VECTOR_COLS = HALF - SCALAR_COLS
 
+MX_ALIGN = 256
 LAST_WIDTHS = (256, 128, 128)
 WARM_MATMULS = 8
 
@@ -97,7 +98,7 @@ def tile_pt_grumb_pa_kernel(
         def load_weight_codes(w, g, first=0, width=FEATURES):
             if first == 0:
                 w_codes[(w, g)] = keep.tile(
-                    [P, FEATURES], U32, name="w_codes_%s_%d" % (w, g), align_bytes=64
+                    [P, FEATURES], U32, name="w_codes_%s_%d" % (w, g), align_bytes=MX_ALIGN
                 )
             nc.sync.dma_start(
                 out=w_codes[(w, g)][:, first : first + width].bitcast(I32),
@@ -107,7 +108,7 @@ def tile_pt_grumb_pa_kernel(
             )
 
         def quantise(a, g, h, scalar_helps):
-            grouped = stage.tile([P, HALF, PACK], BF16, align_bytes=64)
+            grouped = stage.tile([P, HALF, PACK], BF16, align_bytes=MX_ALIGN)
             vector_cols = VECTOR_COLS if scalar_helps else HALF
             nc.vector.tensor_copy(
                 out=grouped[:, :vector_cols, :].rearrange("p (c i) t -> p c t i", i=RUN),
@@ -119,10 +120,10 @@ def tile_pt_grumb_pa_kernel(
                     in_=raw[(a, g, h)][:, :, vector_cols:].rearrange("p t (c i) -> p c t i", i=RUN),
                 )
             act_codes[(a, g, h)] = keep.tile(
-                [P, HALF], U32, name="act_codes_%s_%d_%d" % (a, g, h), align_bytes=64
+                [P, HALF], U32, name="act_codes_%s_%d_%d" % (a, g, h), align_bytes=MX_ALIGN
             )
             act_scales[(a, g, h)] = keep.tile(
-                [P, HALF], U8, name="act_scales_%s_%d_%d" % (a, g, h), align_bytes=64
+                [P, HALF], U8, name="act_scales_%s_%d_%d" % (a, g, h), align_bytes=MX_ALIGN
             )
             nc.vector.quantize_mx(
                 out=act_codes[(a, g, h)][:].bitcast(FP8X4),
@@ -190,7 +191,7 @@ def tile_pt_grumb_pa_kernel(
                 out=out[n * P : (n + 1) * P, h * HALF : (h + 1) * HALF], in_=result[:]
             )
 
-        w_scales["inp"] = keep.tile([P, FEATURES], U8, name="w_scales_inp", align_bytes=64)
+        w_scales["inp"] = keep.tile([P, FEATURES], U8, name="w_scales_inp", align_bytes=MX_ALIGN)
         nc.vector.memset(w_scales["inp"][:].bitcast(I32), 0)
         warm = keep.tile([P, HALF], BF16, name="warm")
         nc.vector.memset(warm[:], 1.0)
@@ -203,7 +204,7 @@ def tile_pt_grumb_pa_kernel(
             )
 
         for w, a in BLOCK_TERMS[1:] + GATE_TERMS:
-            w_scales[w] = keep.tile([P, FEATURES], U8, name="w_scales_%s" % w, align_bytes=64)
+            w_scales[w] = keep.tile([P, FEATURES], U8, name="w_scales_%s" % w, align_bytes=MX_ALIGN)
             nc.vector.memset(w_scales[w][:].bitcast(I32), 0)
 
         low, high = (0, FEATURES // 2), (FEATURES // 2, FEATURES // 2)

@@ -20,6 +20,7 @@ N_TILES = FEATURES // P
 HALF = 512
 HALVES = BATCH // HALF
 QUADRANTS = 4
+W_PLANE = 4
 RUN = 4
 SCALAR_COLS = HALF // 3 // RUN * RUN
 VECTOR_COLS = HALF - SCALAR_COLS
@@ -91,7 +92,9 @@ def tile_pt_grumb_pa_kernel(
         def load_weight_scales(w, queue, word):
             for quadrant in range(QUADRANTS):
                 queue.dma_start(
-                    out=w_scales[w][32 * quadrant : 32 * quadrant + GROUPS * 4, :].bitcast(word),
+                    out=w_scales[w][
+                        32 * quadrant + W_PLANE : 32 * quadrant + W_PLANE + GROUPS * 4, :
+                    ].bitcast(word),
                     in_=scales_in[w][:, 4 * quadrant : 4 * quadrant + 4, :].bitcast(word),
                 )
 
@@ -143,7 +146,7 @@ def tile_pt_grumb_pa_kernel(
                 nc.tensor.matmul_mx(
                     out=banks[n][:],
                     lhsT=w_codes[(w, g)][:, n_cols].bitcast(FP8X4),
-                    lhsT_scale=w_scales[w][4 * g : P, n_cols],
+                    lhsT_scale=w_scales[w][W_PLANE + 4 * g : P, n_cols],
                     rhs=act_codes[(a, g, h)][:].bitcast(FP8X4),
                     rhs_scale=act_scales[(a, g, h)][:],
                     start=(c == 0),
@@ -166,7 +169,7 @@ def tile_pt_grumb_pa_kernel(
                     nc.tensor.matmul_mx(
                         out=bank[:],
                         lhsT=w_codes[(w, g)][:, n_cols].bitcast(FP8X4),
-                        lhsT_scale=w_scales[w][4 * g : P, n_cols],
+                        lhsT_scale=w_scales[w][W_PLANE + 4 * g : P, n_cols],
                         rhs=act_codes[(a, g, h)][:, cols].bitcast(FP8X4),
                         rhs_scale=act_scales[(a, g, h)][:, cols],
                         start=(c == 0),

from contextlib import ExitStack

import concourse.mybir as mybir

BF16 = mybir.dt.bfloat16
F32 = mybir.dt.float32
I32 = mybir.dt.int32
U32 = mybir.dt.uint32
U8 = mybir.dt.uint8
FP8X4 = mybir.dt.float8_e4m3fn_x4
SIGMOID = mybir.ActivationFunctionType.Sigmoid

P = 128
PACK = 4
K_PASS = P * PACK
FEATURES = 1024
BATCH = 1024
GROUPS = FEATURES // K_PASS
N_TILES = FEATURES // P
HALF = 512
HALVES = BATCH // HALF
QUADRANTS = 4
W_PLANE = 4
RUN = 4
SCALAR_COLS = HALF // 3 // RUN * RUN
VECTOR_COLS = HALF - SCALAR_COLS

MX_ALIGN = 256
LAST_WIDTHS = (256, 128, 128)
WARM_MATMULS = 8

FLOPS = 5 * 2 * FEATURES * FEATURES * BATCH

BLOCK_TERMS = (("inp", "x"), ("rec_inp", "out0"))
GATE_TERMS = (("inpgate", "x"), ("rec_inpgate", "out0"), ("mem_inpgate", "mem0"))


def tile_pt_grumb_pa_kernel(
    tc,
    x,
    out0,
    mem0,
    w_inp_words,
    w_inp_scales,
    w_rec_inp_words,
    w_rec_inp_scales,
    w_inpgate_words,
    w_inpgate_scales,
    w_mem_inpgate_words,
    w_mem_inpgate_scales,
    w_rec_inpgate_words,
    w_rec_inpgate_scales,
    out,
):
    nc = tc.nc
    activations = {"x": x, "out0": out0, "mem0": mem0}
    words_in = {
        "inp": w_inp_words,
        "rec_inp": w_rec_inp_words,
        "inpgate": w_inpgate_words,
        "mem_inpgate": w_mem_inpgate_words,
        "rec_inpgate": w_rec_inpgate_words,
    }
    scales_in = {
        "inp": w_inp_scales,
        "rec_inp": w_rec_inp_scales,
        "inpgate": w_inpgate_scales,
        "mem_inpgate": w_mem_inpgate_scales,
        "rec_inpgate": w_rec_inpgate_scales,
    }

    with ExitStack() as ctx:
        ctx.enter_context(tc.manual_schedule())
        keep = ctx.enter_context(tc.tile_pool(name="keep", bufs=1))
        stage = ctx.enter_context(tc.tile_pool(name="stage", bufs=3))
        psum = ctx.enter_context(tc.psum_pool(name="psum", bufs=8))

        raw = {}
        act_codes = {}
        act_scales = {}
        w_codes = {}
        w_scales = {}
        block_sig = {}

        def load_activation(a, g, h):
            raw[(a, g, h)] = keep.tile([P, PACK, HALF], BF16, name="raw_%s_%d_%d" % (a, g, h))
            rows = activations[a][g * K_PASS : (g + 1) * K_PASS, h * HALF : (h + 1) * HALF]
            nc.sync.dma_start(
                out=raw[(a, g, h)][:], in_=rows.rearrange("(p t) c -> p t c", t=PACK)
            )

        def load_weight_scales(w, queue, word):
            for quadrant in range(QUADRANTS):
                queue.dma_start(
                    out=w_scales[w][
                        32 * quadrant + W_PLANE : 32 * quadrant + W_PLANE + GROUPS * 4, :
                    ].bitcast(word),
                    in_=scales_in[w][:, 4 * quadrant : 4 * quadrant + 4, :].bitcast(word),
                )

        def load_weight_codes(w, g, first=0, width=FEATURES):
            if first == 0:
                w_codes[(w, g)] = keep.tile(
                    [P, FEATURES], U32, name="w_codes_%s_%d" % (w, g), align_bytes=MX_ALIGN
                )
            nc.sync.dma_start(
                out=w_codes[(w, g)][:, first : first + width].bitcast(I32),
                in_=words_in[w][g, :, first : first + width, :]
                .rearrange("p n t -> p (n t)")
                .bitcast(I32),
            )

        def quantise(a, g, h, scalar_helps):
            grouped = stage.tile([P, HALF, PACK], BF16, align_bytes=MX_ALIGN)
            vector_cols = VECTOR_COLS if scalar_helps else HALF
            nc.vector.tensor_copy(
                out=grouped[:, :vector_cols, :].rearrange("p (c i) t -> p c t i", i=RUN),
                in_=raw[(a, g, h)][:, :, :vector_cols].rearrange("p t (c i) -> p c t i", i=RUN),
            )
            if scalar_helps:
                nc.scalar.copy(
                    out=grouped[:, vector_cols:, :].rearrange("p (c i) t -> p c t i", i=RUN),
                    in_=raw[(a, g, h)][:, :, vector_cols:].rearrange("p t (c i) -> p c t i", i=RUN),
                )
            act_codes[(a, g, h)] = keep.tile(
                [P, HALF], U32, name="act_codes_%s_%d_%d" % (a, g, h), align_bytes=MX_ALIGN
            )
            act_scales[(a, g, h)] = keep.tile(
                [P, HALF], U8, name="act_scales_%s_%d_%d" % (a, g, h), align_bytes=MX_ALIGN
            )
            nc.vector.quantize_mx(
                out=act_codes[(a, g, h)][:].bitcast(FP8X4),
                scales=act_scales[(a, g, h)][:],
                in_=grouped[:].rearrange("p c t -> p (c t)"),
            )

        def run_round(terms, h, visits, finish):
            last = len(terms) * GROUPS - 1
            banks = {}
            for n, c in visits:
                w, a = terms[c // GROUPS]
                g = c % GROUPS
                if c == 0:
                    banks[n] = psum.tile([P, HALF], F32, name="bank")
                n_cols = slice(n * P, (n + 1) * P)
                nc.tensor.matmul_mx(
                    out=banks[n][:],
                    lhsT=w_codes[(w, g)][:, n_cols].bitcast(FP8X4),
                    lhsT_scale=w_scales[w][W_PLANE + 4 * g : P, n_cols],
                    rhs=act_codes[(a, g, h)][:].bitcast(FP8X4),
                    rhs_scale=act_scales[(a, g, h)][:],
                    start=(c == 0),
                    stop=(c == last),
                )
                if c == last:
                    finish(n, h, banks[n])

        def run_last_tile(terms, n, h):
            last = len(terms) * GROUPS - 1
            n_cols = slice(n * P, (n + 1) * P)
            first = 0
            for width in LAST_WIDTHS:
                cols = slice(first, first + width)
                bank = psum.tile([P, width], F32, name="bank")
                result = keep.tile([P, width], F32, name="result_%d_%d_%d" % (n, h, first))
                for c in range(last + 1):
                    w, a = terms[c // GROUPS]
                    g = c % GROUPS
                    nc.tensor.matmul_mx(
                        out=bank[:],
                        lhsT=w_codes[(w, g)][:, n_cols].bitcast(FP8X4),
                        lhsT_scale=w_scales[w][W_PLANE + 4 * g : P, n_cols],
                        rhs=act_codes[(a, g, h)][:, cols].bitcast(FP8X4),
                        rhs_scale=act_scales[(a, g, h)][:, cols],
                        start=(c == 0),
                        stop=(c == last),
                    )
                nc.scalar.activation(out=result[:], in_=bank[:], func=SIGMOID)
                nc.vector.tensor_mul(out=result[:], in0=result[:], in1=block_sig[(n, h)][:, cols])
                nc.sync.dma_start(
                    out=out[n_cols, h * HALF + first : h * HALF + first + width], in_=result[:]
                )
                first += width

        def finish_block(n, h, bank):
            block_sig[(n, h)] = keep.tile([P, HALF], F32, name="block_sig_%d_%d" % (n, h))
            nc.scalar.activation(out=block_sig[(n, h)][:], in_=bank[:], func=SIGMOID)

        def finish_gate(n, h, bank):
            result = keep.tile([P, HALF], F32, name="result_%d_%d" % (n, h))
            nc.scalar.activation(out=result[:], in_=bank[:], func=SIGMOID)
            nc.vector.tensor_mul(out=result[:], in0=result[:], in1=block_sig[(n, h)][:])
            nc.sync.dma_start(
                out=out[n * P : (n + 1) * P, h * HALF : (h + 1) * HALF], in_=result[:]
            )

        w_scales["inp"] = keep.tile([P, FEATURES], U8, name="w_scales_inp", align_bytes=MX_ALIGN)
        nc.vector.memset(w_scales["inp"][:].bitcast(I32), 0)
        warm = keep.tile([P, HALF], BF16, name="warm")
        nc.vector.memset(warm[:], 1.0)
        warm_sig = keep.tile([P, 1], F32, name="warm_sig")
        nc.scalar.activation(out=warm_sig[:], in_=warm[:, 0:1], func=SIGMOID)
        warm_bank = psum.tile([P, HALF], F32, name="bank")
        for i in range(WARM_MATMULS):
            nc.tensor.matmul(
                out=warm_bank[:], lhsT=warm[:, :P], rhs=warm[:], start=True, stop=True
            )

        for w, a in BLOCK_TERMS[1:] + GATE_TERMS:
            w_scales[w] = keep.tile([P, FEATURES], U8, name="w_scales_%s" % w, align_bytes=MX_ALIGN)
            nc.vector.memset(w_scales[w][:].bitcast(I32), 0)

        low, high = (0, FEATURES // 2), (FEATURES // 2, FEATURES // 2)
        load_activation("x", 0, 0)
        load_weight_codes("inp", 0, *low)
        load_weight_scales("inp", nc.sync, I32)
        for w in ("rec_inp", "inpgate", "rec_inpgate", "mem_inpgate"):
            load_weight_scales(w, nc.gpsimd, F32)
        load_activation("x", 1, 0)
        load_weight_codes("inp", 0, *high)
        load_weight_codes("inp", 1, *low)
        load_activation("out0", 0, 0)
        load_weight_codes("inp", 1, *high)
        load_weight_codes("rec_inp", 0, *low)
        load_activation("out0", 1, 0)
        load_weight_codes("rec_inp", 0, *high)
        load_weight_codes("rec_inp", 1, *low)
        load_weight_codes("rec_inp", 1, *high)
        for w in ("inpgate", "rec_inpgate"):
            for g in range(GROUPS):
                load_weight_codes(w, g)
        for g in range(GROUPS):
            load_activation("mem0", g, 0)
        for g in range(GROUPS):
            load_weight_codes("mem_inpgate", g)
        for a in ("x", "out0", "mem0"):
            for g in range(GROUPS):
                load_activation(a, g, 1)

        for h in range(HALVES):
            for a in ("x", "out0", "mem0"):
                for g in range(GROUPS):
                    quantise(a, g, h, scalar_helps=(h == 0 and a != "mem0"))

        tiles = range(N_TILES)
        run_round(
            BLOCK_TERMS,
            0,
            [(n, c) for c in range(len(BLOCK_TERMS) * GROUPS) for n in tiles],
            finish_block,
        )
        run_round(
            GATE_TERMS,
            0,
            [(n, GROUPS * t + g) for t in range(len(GATE_TERMS)) for n in tiles for g in range(GROUPS)],
            finish_gate,
        )
        run_round(
            BLOCK_TERMS,
            1,
            [(n, GROUPS * t + g) for t in range(len(BLOCK_TERMS)) for n in tiles for g in range(GROUPS)],
            finish_block,
        )
        run_round(
            GATE_TERMS,
            1,
            [(n, c) for n in tiles[:-1] for c in range(len(GATE_TERMS) * GROUPS)],
            finish_gate,
        )
        run_last_tile(GATE_TERMS, tiles[-1], 1)
